import numpy as np
import ml_dtypes


def mxq(x, axis, fmt="e4m3"):
    dtype, down = {"e4m3": (ml_dtypes.float8_e4m3fn, 7), "e5m2": (ml_dtypes.float8_e5m2, 14)}[fmt]
    v = np.moveaxis(np.asarray(x, np.float32).astype(ml_dtypes.bfloat16).astype(np.float64), axis, -1)
    blocks = v.reshape(v.shape[:-1] + (-1, 32))
    amax = np.abs(blocks).max(-1, keepdims=True)
    byte = np.maximum(np.where(amax > 0, np.frexp(amax)[1] - 1 + 127, 0) - down, 1)
    scale = np.exp2(byte - 127.0)
    codes = (blocks / scale).astype(np.float32).astype(dtype).astype(np.float64)
    return np.moveaxis((codes * scale).reshape(v.shape), -1, axis)


WIDE = False


def mx_kscale(k):
    if not WIDE:
        return np.ones(k)
    levels = np.array([10, -10, 5, -5, 0])
    a = np.random.permutation(np.resize(levels, k // 512 * 4)).reshape(k // 512, 4)
    idx = np.arange(k)
    return np.exp2(a[idx // 512, idx % 128 // 32])


BF16 = ml_dtypes.bfloat16


def bf(x):
    return np.asarray(x, np.float32).astype(BF16)


def f64(x):
    return np.asarray(x).astype(np.float64)


E2M1 = np.array([0.0, 0.5, 1.0, 1.5, 2.0, 3.0, 4.0, 6.0, -0.0, -0.5, -1.0, -1.5, -2.0, -3.0, -4.0, -6.0])


def pack_weight(w, fmt):
    k, n = w.shape
    w = f64(bf(w)).reshape(k // 32, 32, n)
    amax = np.abs(w).max(1)
    if fmt == "e4m3":
        byte = np.frexp(amax)[1] - 1 + 127 - 7
    else:
        mant, ex = np.frexp(amax / 6.0)
        byte = np.where(mant > 0.5, ex, ex - 1) + 127
    byte = np.clip(np.where(amax > 0, byte, 1), 1, 254)
    scaled = (w * np.exp2(127.0 - byte)[:, None, :]).reshape(k, n).astype(np.float32)
    by_word = np.ascontiguousarray(scaled.reshape(k // 512, 128, 4, n).transpose(0, 1, 3, 2))
    if fmt == "e4m3":
        words = by_word.astype(ml_dtypes.float8_e4m3fn).view(np.uint8)
    else:
        c = by_word.astype(ml_dtypes.float4_e2m1fn).view(np.uint8) & 0xF
        words = c[..., 0::2] | (c[..., 1::2] << 4)
    return np.ascontiguousarray(words), np.ascontiguousarray(byte.astype(np.uint8).reshape(k // 512, 16, n))


def unpack_weight(words, scales, fmt):
    g, p, n, _ = words.shape
    if fmt == "e4m3":
        vals = np.ascontiguousarray(words).view(ml_dtypes.float8_e4m3fn).astype(np.float64)
    else:
        nib = np.empty((g, p, n, 4), np.uint8)
        nib[..., 0::2] = words & 0xF
        nib[..., 1::2] = words >> 4
        vals = E2M1[nib]
    vals = vals * np.repeat(np.exp2(scales.astype(np.float64) - 127.0), 8, axis=1)[..., None]
    return vals.transpose(0, 1, 3, 2).reshape(g * 512, n)

def pack4(w):
    words, scales = pack_weight(w, "e2m1")
    return words.reshape(words.shape[0], 128, -1), scales


def unpack4(words, scales):
    return unpack_weight(words.reshape(words.shape[0], 128, -1, 2), scales, "e2m1")


B, N, D, A = 4, 1024, 512, 128
K = D + D
NB = N // A


def setup_inputs():
    st = mx_kscale(K)
    s, t = st[:D], st[D:]
    data = bf(np.random.standard_normal((B, N, D)) * 2.0 * s)
    pooled = bf(np.random.standard_normal((B, N, A)) * 0.37 / np.sqrt(NB))
    W_abs = bf(np.random.standard_normal((A, D)) * 3.0 * np.sqrt(NB / A) * t)
    words, scales = pack4(np.random.standard_normal((K, D)) * 0.5 / np.sqrt(D) / st[:, None])
    return {"data": data,
            "pooled": pooled,
            "W_abs": W_abs,
            "W_merge_words": words,
            "W_merge_scales": scales}


def reference(data, pooled, W_abs, W_merge_words, W_merge_scales):
    abstract = f64(pooled) @ f64(W_abs)
    x = np.concatenate([f64(data), abstract], axis=-1)
    return mxq(x, 2, "e4m3") @ unpack4(W_merge_words, W_merge_scales)

@@ -1,0 +1,176 @@
+from contextlib import ExitStack
+
+import concourse.mybir as mybir
+from concourse.masks import make_identity
+
+BF16 = mybir.dt.bfloat16
+F32 = mybir.dt.float32
+I32 = mybir.dt.int32
+U32 = mybir.dt.uint32
+U8 = mybir.dt.uint8
+FP8X4 = mybir.dt.float8_e4m3fn_x4
+FP4X4 = mybir.dt.float4_e2m1fn_x4
+
+P = 128
+PACK = 4
+TOKENS = 4 * 1024
+D = 512
+A = 128
+N_OUT = 512
+PASSES = 2
+TILES = TOKENS // P
+ROUND_TILES = 4
+ROUNDS = TILES // ROUND_TILES
+ROUND_TOKENS = ROUND_TILES * P
+BANK_TILES = 2
+BANK_TOKENS = BANK_TILES * P
+ROUND_BANKS = ROUND_TILES // BANK_TILES
+POOLED_CHUNK = 8
+POOLED_CHUNKS = TILES // POOLED_CHUNK
+
+FLOPS = 2 * TOKENS * A * D + 2 * TOKENS * (PASSES * D) * N_OUT
+
+
+def copy_by_turns(nc, turn, out, in_):
+    if turn % 2 == 0:
+        nc.scalar.copy(out=out, in_=in_)
+    else:
+        nc.vector.tensor_copy(out=out, in_=in_)
+
+
+def tile_abstraction_pb_kernel(tc, data, pooled, W_abs, W_merge_words, W_merge_scales, out):
+    nc = tc.nc
+    data_rows = data.flatten_outer_dims().rearrange("(p i) k -> p i k", i=TILES)
+    pooled_rows = pooled.flatten_outer_dims().rearrange("(p i) a -> p i a", i=TILES)
+    out_rows = out.flatten_outer_dims().rearrange("(p i) n -> p i n", i=TILES)
+
+    with ExitStack() as ctx:
+        ctx.enter_context(tc.manual_schedule())
+        keep = ctx.enter_context(tc.tile_pool(name="keep", bufs=1))
+        work = ctx.enter_context(tc.tile_pool(name="work", bufs=3))
+        psum_data = ctx.enter_context(tc.psum_pool(name="psum_data", bufs=2))
+        psum_abs = ctx.enter_context(tc.psum_pool(name="psum_abs", bufs=2))
+        psum_out = ctx.enter_context(tc.psum_pool(name="psum_out", bufs=4))
+
+        w_planes = keep.tile([P, PASSES, N_OUT], U8, name="w_planes", align_bytes=64)
+        nc.vector.memset(w_planes[:].bitcast(I32), 0)
+        ident_bf16 = keep.tile([P, P], BF16, name="ident_bf16")
+        make_identity(nc, ident_bf16[:])
+        ident_f32 = keep.tile([P, P], F32, name="ident_f32")
+        make_identity(nc, ident_f32[:])
+
+        pooled_sb = []
+        for c in range(POOLED_CHUNKS):
+            pooled_sb.append(keep.tile([P, POOLED_CHUNK, A], BF16, name="pooled%d" % c))
+        data_sb = []
+        for r in range(ROUNDS):
+            data_sb.append(keep.tile([P, ROUND_TILES, D], BF16, name="data%d" % r))
+        w_abs_sb = keep.tile([A, D], BF16, name="w_abs_sb")
+        w_words = keep.tile([P, PASSES, 2 * N_OUT], U8, name="w_words", align_bytes=64)
+
+        def load_pooled(c):
+            tiles = slice(c * POOLED_CHUNK, (c + 1) * POOLED_CHUNK)
+            nc.sync.dma_start(out=pooled_sb[c][:], in_=pooled_rows[:, tiles, :])
+
+        def load_data(r):
+            tiles = slice(r * ROUND_TILES, (r + 1) * ROUND_TILES)
+            nc.sync.dma_start(out=data_sb[r][:], in_=data_rows[:, tiles, :])
+
+        load_pooled(0)
+        nc.sync.dma_start(out=w_abs_sb[:], in_=W_abs)
+        for c in range(1, POOLED_CHUNKS):
+            load_pooled(c)
+        load_data(0)
+        load_data(1)
+        nc.sync.dma_start(
+            out=w_words[:].bitcast(I32),
+            in_=W_merge_words.bitcast(I32).rearrange("g p w -> p g w"),
+        )
+        scale_rows = W_merge_scales.bitcast(I32).rearrange("g (q s) w -> s q g w", s=4)
+        for s in range(4):
+            nc.sync.dma_start(out=w_planes[:].bitcast(I32)[s:P:32, :, :], in_=scale_rows[s])
+        for r in range(2, ROUNDS):
+            load_data(r)
+
+        w_abs_by_t = keep.tile([A, PACK, P], BF16, name="w_abs_by_t")
+        nc.vector.tensor_copy(out=w_abs_by_t[:], in_=w_abs_sb[:].rearrange("a (p t) -> a t p", t=PACK))
+
+        pooled_t = []
+        for c in range(POOLED_CHUNKS):
+            pooled_t_ps = psum_out.tile([A, POOLED_CHUNK, P], BF16, name="pooled_t_ps", tag="bank")
+            for j in range(POOLED_CHUNK):
+                nc.tensor.transpose(out=pooled_t_ps[:, j, :], in_=pooled_sb[c][:, j, :], identity=ident_bf16[:])
+            pooled_t.append(keep.tile([A, POOLED_CHUNK, P], BF16, name="pooled_t%d" % c))
+            copy_by_turns(nc, c, out=pooled_t[c][:], in_=pooled_t_ps[:])
+
+        def prepare(r):
+            grouped = work.tile([P, PASSES, ROUND_TOKENS, PACK], BF16, name="grouped", align_bytes=64)
+            x_words = work.tile([P, PASSES, ROUND_TOKENS], U32, name="x_words", align_bytes=64)
+            x_planes = work.tile([P, PASSES, ROUND_TOKENS], U8, name="x_planes", align_bytes=64)
+
+            for b in range(ROUND_BANKS):
+                data_t_ps = psum_data.tile([P, BANK_TILES, 2, P], F32, name="data_t_ps")
+                for j in range(BANK_TILES):
+                    words = data_sb[r][:, b * BANK_TILES + j, :].bitcast(F32)
+                    for u in range(2):
+                        nc.tensor.transpose(
+                            out=data_t_ps[:, j, u, :], in_=words[:, u : D // 2 : 2], identity=ident_f32[:]
+                        )
+                tokens = slice(b * BANK_TOKENS, (b + 1) * BANK_TOKENS)
+                nc.vector.tensor_copy(
+                    out=grouped[:, 0, tokens, :].bitcast(F32).rearrange("p (j m) u -> p j m u", j=BANK_TILES),
+                    in_=data_t_ps[:].rearrange("p j u m -> p j m u"),
+                )
+            nc.vector.quantize_mx(
+                out=x_words[:, 0, :].bitcast(FP8X4),
+                scales=x_planes[:, 0, :],
+                in_=grouped[:, 0, :, :].rearrange("p m t -> p (m t)"),
+            )
+
+            for b in range(ROUND_BANKS):
+                first_tile = r * ROUND_TILES + b * BANK_TILES
+                chunk = pooled_t[first_tile // POOLED_CHUNK]
+                in_chunk = first_tile % POOLED_CHUNK
+                abs_t_ps = psum_abs.tile([P, PACK, BANK_TOKENS], BF16, name="abs_t_ps")
+                for t in range(PACK):
+                    nc.tensor.matmul(
+                        out=abs_t_ps[:, t, :],
+                        lhsT=w_abs_by_t[:, t, :],
+                        rhs=chunk[:, in_chunk : in_chunk + BANK_TILES, :].rearrange("a j m -> a (j m)"),
+                        start=True,
+                        stop=True,
+                    )
+                tokens = slice(b * BANK_TOKENS, (b + 1) * BANK_TOKENS)
+                nc.scalar.copy(out=grouped[:, 1, tokens, :], in_=abs_t_ps[:].rearrange("p t m -> p m t"))
+            nc.vector.quantize_mx(
+                out=x_words[:, 1, :].bitcast(FP8X4),
+                scales=x_planes[:, 1, :],
+                in_=grouped[:, 1, :, :].rearrange("p m t -> p (m t)"),
+            )
+            return x_words, x_planes
+
+        def merge(r, x_words, x_planes):
+            for b in range(ROUND_BANKS):
+                first_tile = r * ROUND_TILES + b * BANK_TILES
+                out_sb = keep.tile([P, BANK_TILES, N_OUT], F32, name="out%d" % (first_tile // BANK_TILES))
+                for j in range(BANK_TILES):
+                    tokens = slice((b * BANK_TILES + j) * P, (b * BANK_TILES + j + 1) * P)
+                    out_ps = psum_out.tile([P, N_OUT], F32, name="out_ps", tag="bank")
+                    for g in range(PASSES):
+                        nc.tensor.matmul_mx(
+                            out=out_ps[:],
+                            lhsT=x_words[:, g, tokens].bitcast(FP8X4),
+                            lhsT_scale=x_planes[:, g, tokens],
+                            rhs=w_words[:, g, :].bitcast(FP4X4),
+                            rhs_scale=w_planes[:, g, :],
+                            start=(g == 0),
+                            stop=(g == PASSES - 1),
+                        )
+                    copy_by_turns(nc, j, out=out_sb[:, j, :], in_=out_ps[:])
+                nc.sync.dma_start(out=out_rows[:, first_tile : first_tile + BANK_TILES, :], in_=out_sb[:])
+
+        ready = prepare(0)
+        for r in range(ROUNDS):
+            following = prepare(r + 1) if r + 1 < ROUNDS else None
+            merge(r, ready[0], ready[1])
+            ready = following

@@ -25,8 +25,8 @@ ROUND_TOKENS = ROUND_TILES * P
 BANK_TILES = 2
 BANK_TOKENS = BANK_TILES * P
 ROUND_BANKS = ROUND_TILES // BANK_TILES
-POOLED_CHUNK = 8
-POOLED_CHUNKS = TILES // POOLED_CHUNK
+POOLED_ROUNDS = 2
+POOLED_LOADS = ROUNDS // POOLED_ROUNDS
 
 FLOPS = 2 * TOKENS * A * D + 2 * TOKENS * (PASSES * D) * N_OUT
 
@@ -60,8 +60,8 @@ def tile_abstraction_pb_kernel(tc, data, pooled, W_abs, W_merge_words, W_merge_s
         make_identity(nc, ident_f32[:])
 
         pooled_sb = []
-        for c in range(POOLED_CHUNKS):
-            pooled_sb.append(keep.tile([P, POOLED_CHUNK, A], BF16, name="pooled%d" % c))
+        for c in range(POOLED_LOADS):
+            pooled_sb.append(keep.tile([P, POOLED_ROUNDS * ROUND_TILES, A], BF16, name="pooled%d" % c))
         data_sb = []
         for r in range(ROUNDS):
             data_sb.append(keep.tile([P, ROUND_TILES, D], BF16, name="data%d" % r))
@@ -69,7 +69,7 @@ def tile_abstraction_pb_kernel(tc, data, pooled, W_abs, W_merge_words, W_merge_s
         w_words = keep.tile([P, PASSES, 2 * N_OUT], U8, name="w_words", align_bytes=64)
 
         def load_pooled(c):
-            tiles = slice(c * POOLED_CHUNK, (c + 1) * POOLED_CHUNK)
+            tiles = slice(c * POOLED_ROUNDS * ROUND_TILES, (c + 1) * POOLED_ROUNDS * ROUND_TILES)
             nc.sync.dma_start(out=pooled_sb[c][:], in_=pooled_rows[:, tiles, :])
 
         def load_data(r):
@@ -78,10 +78,9 @@ def tile_abstraction_pb_kernel(tc, data, pooled, W_abs, W_merge_words, W_merge_s
 
         load_pooled(0)
         nc.sync.dma_start(out=w_abs_sb[:], in_=W_abs)
-        for c in range(1, POOLED_CHUNKS):
-            load_pooled(c)
-        load_data(0)
-        load_data(1)
+        for r in range(POOLED_ROUNDS):
+            load_data(r)
+        load_pooled(1)
         nc.sync.dma_start(
             out=w_words[:].bitcast(I32),
             in_=W_merge_words.bitcast(I32).rearrange("g p w -> p g w"),
@@ -89,19 +88,35 @@ def tile_abstraction_pb_kernel(tc, data, pooled, W_abs, W_merge_words, W_merge_s
         scale_rows = W_merge_scales.bitcast(I32).rearrange("g (q s) w -> s q g w", s=4)
         for s in range(4):
             nc.sync.dma_start(out=w_planes[:].bitcast(I32)[s:P:32, :, :], in_=scale_rows[s])
-        for r in range(2, ROUNDS):
-            load_data(r)
+        for c in range(1, POOLED_LOADS):
+            for r in range(c * POOLED_ROUNDS, (c + 1) * POOLED_ROUNDS):
+                load_data(r)
+            if c + 1 < POOLED_LOADS:
+                load_pooled(c + 1)
 
         w_abs_by_t = keep.tile([A, PACK, P], BF16, name="w_abs_by_t")
         nc.vector.tensor_copy(out=w_abs_by_t[:], in_=w_abs_sb[:].rearrange("a (p t) -> a t p", t=PACK))
 
-        pooled_t = []
-        for c in range(POOLED_CHUNKS):
-            pooled_t_ps = psum_out.tile([A, POOLED_CHUNK, P], BF16, name="pooled_t_ps", tag="bank")
-            for j in range(POOLED_CHUNK):
-                nc.tensor.transpose(out=pooled_t_ps[:, j, :], in_=pooled_sb[c][:, j, :], identity=ident_bf16[:])
-            pooled_t.append(keep.tile([A, POOLED_CHUNK, P], BF16, name="pooled_t%d" % c))
-            copy_by_turns(nc, c, out=pooled_t[c][:], in_=pooled_t_ps[:])
+        def transpose_pooled(r):
+            rows = pooled_sb[r // POOLED_ROUNDS]
+            first = (r % POOLED_ROUNDS) * ROUND_TILES
+            pooled_t_ps = psum_out.tile([A, ROUND_TILES, P], BF16, name="pooled_t_ps", tag="bank")
+            for j in range(ROUND_TILES):
+                nc.tensor.transpose(out=pooled_t_ps[:, j, :], in_=rows[:, first + j, :], identity=ident_bf16[:])
+            transposed = work.tile([A, ROUND_TOKENS], BF16, name="transposed")
+            nc.scalar.copy(out=transposed[:], in_=pooled_t_ps[:].rearrange("a j m -> a (j m)"))
+            return transposed
+
+        def sort_words(r):
+            by_half = work.tile([P, ROUND_TILES, 2, P], F32, name="by_half")
+            nc.vector.tensor_copy(
+                out=by_half[:], in_=data_sb[r][:].bitcast(F32).rearrange("m j (p u) -> m j u p", u=2)
+            )
+            return by_half
+
+        pooled_t = {0: transpose_pooled(0), 1: transpose_pooled(1)}
+        data_words = {0: sort_words(0)}
+        x_mx = {}
 
         def prepare(r):
             grouped = work.tile([P, PASSES, ROUND_TOKENS, PACK], BF16, name="grouped", align_bytes=64)
@@ -109,68 +124,68 @@ def tile_abstraction_pb_kernel(tc, data, pooled, W_abs, W_merge_words, W_merge_s
             x_planes = work.tile([P, PASSES, ROUND_TOKENS], U8, name="x_planes", align_bytes=64)
 
             for b in range(ROUND_BANKS):
-                data_t_ps = psum_data.tile([P, BANK_TILES, 2, P], F32, name="data_t_ps")
-                for j in range(BANK_TILES):
-                    words = data_sb[r][:, b * BANK_TILES + j, :].bitcast(F32)
-                    for u in range(2):
-                        nc.tensor.transpose(
-                            out=data_t_ps[:, j, u, :], in_=words[:, u : D // 2 : 2], identity=ident_f32[:]
-                        )
                 tokens = slice(b * BANK_TOKENS, (b + 1) * BANK_TOKENS)
-                nc.vector.tensor_copy(
-                    out=grouped[:, 0, tokens, :].bitcast(F32).rearrange("p (j m) u -> p j m u", j=BANK_TILES),
-                    in_=data_t_ps[:].rearrange("p j u m -> p j m u"),
-                )
-            nc.vector.quantize_mx(
-                out=x_words[:, 0, :].bitcast(FP8X4),
-                scales=x_planes[:, 0, :],
-                in_=grouped[:, 0, :, :].rearrange("p m t -> p (m t)"),
-            )
-
-            for b in range(ROUND_BANKS):
-                first_tile = r * ROUND_TILES + b * BANK_TILES
-                chunk = pooled_t[first_tile // POOLED_CHUNK]
-                in_chunk = first_tile % POOLED_CHUNK
                 abs_t_ps = psum_abs.tile([P, PACK, BANK_TOKENS], BF16, name="abs_t_ps")
                 for t in range(PACK):
                     nc.tensor.matmul(
                         out=abs_t_ps[:, t, :],
                         lhsT=w_abs_by_t[:, t, :],
-                        rhs=chunk[:, in_chunk : in_chunk + BANK_TILES, :].rearrange("a j m -> a (j m)"),
+                        rhs=pooled_t[r][:, tokens],
                         start=True,
                         stop=True,
                     )
-                tokens = slice(b * BANK_TOKENS, (b + 1) * BANK_TOKENS)
                 nc.scalar.copy(out=grouped[:, 1, tokens, :], in_=abs_t_ps[:].rearrange("p t m -> p m t"))
-            nc.vector.quantize_mx(
-                out=x_words[:, 1, :].bitcast(FP8X4),
-                scales=x_planes[:, 1, :],
-                in_=grouped[:, 1, :, :].rearrange("p m t -> p (m t)"),
-            )
-            return x_words, x_planes
 
-        def merge(r, x_words, x_planes):
             for b in range(ROUND_BANKS):
-                first_tile = r * ROUND_TILES + b * BANK_TILES
-                out_sb = keep.tile([P, BANK_TILES, N_OUT], F32, name="out%d" % (first_tile // BANK_TILES))
+                tokens = slice(b * BANK_TOKENS, (b + 1) * BANK_TOKENS)
+                data_t_ps = psum_data.tile([P, BANK_TILES, 2, P], F32, name="data_t_ps")
                 for j in range(BANK_TILES):
-                    tokens = slice((b * BANK_TILES + j) * P, (b * BANK_TILES + j + 1) * P)
-                    out_ps = psum_out.tile([P, N_OUT], F32, name="out_ps", tag="bank")
-                    for g in range(PASSES):
-                        nc.tensor.matmul_mx(
-                            out=out_ps[:],
-                            lhsT=x_words[:, g, tokens].bitcast(FP8X4),
-                            lhsT_scale=x_planes[:, g, tokens],
-                            rhs=w_words[:, g, :].bitcast(FP4X4),
-                            rhs_scale=w_planes[:, g, :],
-                            start=(g == 0),
-                            stop=(g == PASSES - 1),
+                    for u in range(2):
+                        nc.tensor.transpose(
+                            out=data_t_ps[:, j, u, :],
+                            in_=data_words[r][:, b * BANK_TILES + j, u, :],
+                            identity=ident_f32[:],
                         )
-                    copy_by_turns(nc, j, out=out_sb[:, j, :], in_=out_ps[:])
-                nc.sync.dma_start(out=out_rows[:, first_tile : first_tile + BANK_TILES, :], in_=out_sb[:])
+                nc.vector.tensor_copy(
+                    out=grouped[:, 0, tokens, :].bitcast(F32).rearrange("p (j m) u -> p j m u", j=BANK_TILES),
+                    in_=data_t_ps[:].rearrange("p j u m -> p j m u"),
+                )
 
-        ready = prepare(0)
+            if r + 2 < ROUNDS:
+                pooled_t[r + 2] = transpose_pooled(r + 2)
+            if r + 1 < ROUNDS:
+                data_words[r + 1] = sort_words(r + 1)
+
+            for g in range(PASSES):
+                nc.vector.quantize_mx(
+                    out=x_words[:, g, :].bitcast(FP8X4),
+                    scales=x_planes[:, g, :],
+                    in_=grouped[:, g, :, :].rearrange("p m t -> p (m t)"),
+                )
+            x_mx[r] = (x_words, x_planes)
+
+        def merge(r):
+            x_words, x_planes = x_mx[r]
+            for j in range(ROUND_TILES):
+                tokens = slice(j * P, (j + 1) * P)
+                out_ps = psum_out.tile([P, N_OUT], F32, name="out_ps", tag="bank")
+                for g in range(PASSES):
+                    nc.tensor.matmul_mx(
+                        out=out_ps[:],
+                        lhsT=x_words[:, g, tokens].bitcast(FP8X4),
+                        lhsT_scale=x_planes[:, g, tokens],
+                        rhs=w_words[:, g, :].bitcast(FP4X4),
+                        rhs_scale=w_planes[:, g, :],
+                        start=(g == 0),
+                        stop=(g == PASSES - 1),
+                    )
+                token_tile = r * ROUND_TILES + j
+                out_sb = keep.tile([P, N_OUT], F32, name="out%d" % token_tile)
+                copy_by_turns(nc, j, out=out_sb[:], in_=out_ps[:])
+                nc.sync.dma_start(out=out_rows[:, token_tile, :], in_=out_sb[:])
+
+        prepare(0)
         for r in range(ROUNDS):
-            following = prepare(r + 1) if r + 1 < ROUNDS else None
-            merge(r, ready[0], ready[1])
-            ready = following
+            if r + 1 < ROUNDS:
+                prepare(r + 1)
+            merge(r)

@@ -25,8 +25,8 @@ ROUND_TOKENS = ROUND_TILES * P
 BANK_TILES = 2
 BANK_TOKENS = BANK_TILES * P
 ROUND_BANKS = ROUND_TILES // BANK_TILES
-POOLED_ROUNDS = 2
-POOLED_LOADS = ROUNDS // POOLED_ROUNDS
+POOLED_AHEAD = 2
+LAST_TILE_GROUPS = 4
 
 FLOPS = 2 * TOKENS * A * D + 2 * TOKENS * (PASSES * D) * N_OUT
 
@@ -48,6 +48,7 @@ def tile_abstraction_pb_kernel(tc, data, pooled, W_abs, W_merge_words, W_merge_s
         ctx.enter_context(tc.manual_schedule())
         keep = ctx.enter_context(tc.tile_pool(name="keep", bufs=1))
         work = ctx.enter_context(tc.tile_pool(name="work", bufs=3))
+        sorted_pool = ctx.enter_context(tc.tile_pool(name="sorted_pool", bufs=2 * ROUND_BANKS))
         psum_data = ctx.enter_context(tc.psum_pool(name="psum_data", bufs=2))
         psum_abs = ctx.enter_context(tc.psum_pool(name="psum_abs", bufs=2))
         psum_out = ctx.enter_context(tc.psum_pool(name="psum_out", bufs=4))
@@ -59,28 +60,30 @@ def tile_abstraction_pb_kernel(tc, data, pooled, W_abs, W_merge_words, W_merge_s
         ident_f32 = keep.tile([P, P], F32, name="ident_f32")
         make_identity(nc, ident_f32[:])
 
-        pooled_sb = []
-        for c in range(POOLED_LOADS):
-            pooled_sb.append(keep.tile([P, POOLED_ROUNDS * ROUND_TILES, A], BF16, name="pooled%d" % c))
-        data_sb = []
-        for r in range(ROUNDS):
-            data_sb.append(keep.tile([P, ROUND_TILES, D], BF16, name="data%d" % r))
+        pooled_sb = [keep.tile([P, ROUND_TILES, A], BF16, name="pooled%d" % r) for r in range(ROUNDS)]
+        data_sb = [
+            [keep.tile([P, BANK_TILES, D], BF16, name="data%d_%d" % (r, b)) for b in range(ROUND_BANKS)]
+            for r in range(ROUNDS)
+        ]
         w_abs_sb = keep.tile([A, D], BF16, name="w_abs_sb")
         w_words = keep.tile([P, PASSES, 2 * N_OUT], U8, name="w_words", align_bytes=64)
 
-        def load_pooled(c):
-            tiles = slice(c * POOLED_ROUNDS * ROUND_TILES, (c + 1) * POOLED_ROUNDS * ROUND_TILES)
-            nc.sync.dma_start(out=pooled_sb[c][:], in_=pooled_rows[:, tiles, :])
-
-        def load_data(r):
+        def load_pooled(r):
             tiles = slice(r * ROUND_TILES, (r + 1) * ROUND_TILES)
-            nc.sync.dma_start(out=data_sb[r][:], in_=data_rows[:, tiles, :])
+            nc.sync.dma_start(out=pooled_sb[r][:], in_=pooled_rows[:, tiles, :])
+
+        def load_round(r):
+            for b in range(ROUND_BANKS):
+                first_tile = r * ROUND_TILES + b * BANK_TILES
+                nc.sync.dma_start(out=data_sb[r][b][:], in_=data_rows[:, first_tile : first_tile + BANK_TILES, :])
+            if r + POOLED_AHEAD < ROUNDS:
+                load_pooled(r + POOLED_AHEAD)
 
         load_pooled(0)
         nc.sync.dma_start(out=w_abs_sb[:], in_=W_abs)
-        for r in range(POOLED_ROUNDS):
-            load_data(r)
         load_pooled(1)
+        load_round(0)
+        load_round(1)
         nc.sync.dma_start(
             out=w_words[:].bitcast(I32),
             in_=W_merge_words.bitcast(I32).rearrange("g p w -> p g w"),
@@ -88,31 +91,29 @@ def tile_abstraction_pb_kernel(tc, data, pooled, W_abs, W_merge_words, W_merge_s
         scale_rows = W_merge_scales.bitcast(I32).rearrange("g (q s) w -> s q g w", s=4)
         for s in range(4):
             nc.sync.dma_start(out=w_planes[:].bitcast(I32)[s:P:32, :, :], in_=scale_rows[s])
-        for c in range(1, POOLED_LOADS):
-            for r in range(c * POOLED_ROUNDS, (c + 1) * POOLED_ROUNDS):
-                load_data(r)
-            if c + 1 < POOLED_LOADS:
-                load_pooled(c + 1)
+        for r in range(2, ROUNDS):
+            load_round(r)
 
         w_abs_by_t = keep.tile([A, PACK, P], BF16, name="w_abs_by_t")
         nc.vector.tensor_copy(out=w_abs_by_t[:], in_=w_abs_sb[:].rearrange("a (p t) -> a t p", t=PACK))
 
         def transpose_pooled(r):
-            rows = pooled_sb[r // POOLED_ROUNDS]
-            first = (r % POOLED_ROUNDS) * ROUND_TILES
             pooled_t_ps = psum_out.tile([A, ROUND_TILES, P], BF16, name="pooled_t_ps", tag="bank")
             for j in range(ROUND_TILES):
-                nc.tensor.transpose(out=pooled_t_ps[:, j, :], in_=rows[:, first + j, :], identity=ident_bf16[:])
+                nc.tensor.transpose(out=pooled_t_ps[:, j, :], in_=pooled_sb[r][:, j, :], identity=ident_bf16[:])
             transposed = work.tile([A, ROUND_TOKENS], BF16, name="transposed")
             nc.scalar.copy(out=transposed[:], in_=pooled_t_ps[:].rearrange("a j m -> a (j m)"))
             return transposed
 
         def sort_words(r):
-            by_half = work.tile([P, ROUND_TILES, 2, P], F32, name="by_half")
-            nc.vector.tensor_copy(
-                out=by_half[:], in_=data_sb[r][:].bitcast(F32).rearrange("m j (p u) -> m j u p", u=2)
-            )
-            return by_half
+            banks = []
+            for b in range(ROUND_BANKS):
+                by_half = sorted_pool.tile([P, BANK_TILES, 2, P], F32, name="by_half")
+                nc.vector.tensor_copy(
+                    out=by_half[:], in_=data_sb[r][b][:].bitcast(F32).rearrange("m j (p u) -> m j u p", u=2)
+                )
+                banks.append(by_half)
+            return banks
 
         pooled_t = {0: transpose_pooled(0), 1: transpose_pooled(1)}
         data_words = {0: sort_words(0)}
@@ -123,7 +124,7 @@ def tile_abstraction_pb_kernel(tc, data, pooled, W_abs, W_merge_words, W_merge_s
             x_words = work.tile([P, PASSES, ROUND_TOKENS], U32, name="x_words", align_bytes=64)
             x_planes = work.tile([P, PASSES, ROUND_TOKENS], U8, name="x_planes", align_bytes=64)
 
-            for b in range(ROUND_BANKS):
+            def abstract_bank(b):
                 tokens = slice(b * BANK_TOKENS, (b + 1) * BANK_TOKENS)
                 abs_t_ps = psum_abs.tile([P, PACK, BANK_TOKENS], BF16, name="abs_t_ps")
                 for t in range(PACK):
@@ -136,26 +137,28 @@ def tile_abstraction_pb_kernel(tc, data, pooled, W_abs, W_merge_words, W_merge_s
                     )
                 nc.scalar.copy(out=grouped[:, 1, tokens, :], in_=abs_t_ps[:].rearrange("p t m -> p m t"))
 
-            for b in range(ROUND_BANKS):
+            def data_bank(b):
                 tokens = slice(b * BANK_TOKENS, (b + 1) * BANK_TOKENS)
                 data_t_ps = psum_data.tile([P, BANK_TILES, 2, P], F32, name="data_t_ps")
                 for j in range(BANK_TILES):
                     for u in range(2):
                         nc.tensor.transpose(
-                            out=data_t_ps[:, j, u, :],
-                            in_=data_words[r][:, b * BANK_TILES + j, u, :],
-                            identity=ident_f32[:],
+                            out=data_t_ps[:, j, u, :], in_=data_words[r][b][:, j, u, :], identity=ident_f32[:]
                         )
                 nc.vector.tensor_copy(
                     out=grouped[:, 0, tokens, :].bitcast(F32).rearrange("p (j m) u -> p j m u", j=BANK_TILES),
                     in_=data_t_ps[:].rearrange("p j u m -> p j m u"),
                 )
 
-            if r + 2 < ROUNDS:
-                pooled_t[r + 2] = transpose_pooled(r + 2)
+            abstract_bank(0)
+            for b in range(ROUND_BANKS):
+                data_bank(b)
+            if r + POOLED_AHEAD < ROUNDS:
+                pooled_t[r + POOLED_AHEAD] = transpose_pooled(r + POOLED_AHEAD)
+            abstract_bank(1)
+
             if r + 1 < ROUNDS:
                 data_words[r + 1] = sort_words(r + 1)
-
             for g in range(PASSES):
                 nc.vector.quantize_mx(
                     out=x_words[:, g, :].bitcast(FP8X4),
@@ -167,22 +170,26 @@ def tile_abstraction_pb_kernel(tc, data, pooled, W_abs, W_merge_words, W_merge_s
         def merge(r):
             x_words, x_planes = x_mx[r]
             for j in range(ROUND_TILES):
-                tokens = slice(j * P, (j + 1) * P)
-                out_ps = psum_out.tile([P, N_OUT], F32, name="out_ps", tag="bank")
-                for g in range(PASSES):
-                    nc.tensor.matmul_mx(
-                        out=out_ps[:],
-                        lhsT=x_words[:, g, tokens].bitcast(FP8X4),
-                        lhsT_scale=x_planes[:, g, tokens],
-                        rhs=w_words[:, g, :].bitcast(FP4X4),
-                        rhs_scale=w_planes[:, g, :],
-                        start=(g == 0),
-                        stop=(g == PASSES - 1),
-                    )
                 token_tile = r * ROUND_TILES + j
+                tokens = slice(j * P, (j + 1) * P)
                 out_sb = keep.tile([P, N_OUT], F32, name="out%d" % token_tile)
-                copy_by_turns(nc, j, out=out_sb[:], in_=out_ps[:])
-                nc.sync.dma_start(out=out_rows[:, token_tile, :], in_=out_sb[:])
+                groups = LAST_TILE_GROUPS if token_tile == TILES - 1 else 1
+                width = N_OUT // groups
+                for c in range(groups):
+                    cols = slice(c * width, (c + 1) * width)
+                    out_ps = psum_out.tile([P, width], F32, name="out_ps", tag="bank")
+                    for g in range(PASSES):
+                        nc.tensor.matmul_mx(
+                            out=out_ps[:],
+                            lhsT=x_words[:, g, tokens].bitcast(FP8X4),
+                            lhsT_scale=x_planes[:, g, tokens],
+                            rhs=w_words[:, g, 2 * c * width : 2 * (c + 1) * width].bitcast(FP4X4),
+                            rhs_scale=w_planes[:, g, cols],
+                            start=(g == 0),
+                            stop=(g == PASSES - 1),
+                        )
+                    copy_by_turns(nc, j + c, out=out_sb[:, cols], in_=out_ps[:])
+                    nc.sync.dma_start(out=out_rows[:, token_tile, cols], in_=out_sb[:, cols])
 
         prepare(0)
         for r in range(ROUNDS):

@@ -31,11 +31,11 @@ LAST_TILE_GROUPS = 4
 FLOPS = 2 * TOKENS * A * D + 2 * TOKENS * (PASSES * D) * N_OUT
 
 
-def copy_by_turns(nc, turn, out, in_):
-    if turn % 2 == 0:
-        nc.scalar.copy(out=out, in_=in_)
-    else:
+def copy_product(nc, turn, out, in_):
+    if (turn % 8) % 3 == 1:
         nc.vector.tensor_copy(out=out, in_=in_)
+    else:
+        nc.scalar.copy(out=out, in_=in_)
 
 
 def tile_abstraction_pb_kernel(tc, data, pooled, W_abs, W_merge_words, W_merge_scales, out):
@@ -188,7 +188,7 @@ def tile_abstraction_pb_kernel(tc, data, pooled, W_abs, W_merge_words, W_merge_s
                             start=(g == 0),
                             stop=(g == PASSES - 1),
                         )
-                    copy_by_turns(nc, j + c, out=out_sb[:, cols], in_=out_ps[:])
+                    copy_product(nc, token_tile + c, out=out_sb[:, cols], in_=out_ps[:])
                     nc.sync.dma_start(out=out_rows[:, token_tile, cols], in_=out_sb[:, cols])
 
         prepare(0)

@@ -32,7 +32,7 @@ FLOPS = 2 * TOKENS * A * D + 2 * TOKENS * (PASSES * D) * N_OUT
 
 
 def copy_product(nc, turn, out, in_):
-    if (turn % 8) % 3 == 1:
+    if turn % 4 == 3 or turn == TILES + 1:
         nc.vector.tensor_copy(out=out, in_=in_)
     else:
         nc.scalar.copy(out=out, in_=in_)

@@ -27,6 +27,7 @@ BANK_TOKENS = BANK_TILES * P
 ROUND_BANKS = ROUND_TILES // BANK_TILES
 POOLED_AHEAD = 2
 LAST_TILE_GROUPS = 4
+WARM_MATMULS = 4
 
 FLOPS = 2 * TOKENS * A * D + 2 * TOKENS * (PASSES * D) * N_OUT
 
@@ -52,6 +53,12 @@ def tile_abstraction_pb_kernel(tc, data, pooled, W_abs, W_merge_words, W_merge_s
         psum_data = ctx.enter_context(tc.psum_pool(name="psum_data", bufs=2))
         psum_abs = ctx.enter_context(tc.psum_pool(name="psum_abs", bufs=2))
         psum_out = ctx.enter_context(tc.psum_pool(name="psum_out", bufs=4))
+
+        zeros = keep.tile([P, N_OUT], BF16, name="zeros")
+        nc.vector.memset(zeros[:], 0.0)
+        warm_ps = psum_out.tile([P, N_OUT], F32, name="warm_ps", tag="bank")
+        for i in range(WARM_MATMULS):
+            nc.tensor.matmul(out=warm_ps[:], lhsT=zeros[:, 0:P], rhs=zeros[:], start=True, stop=True)
 
         w_planes = keep.tile([P, PASSES, N_OUT], U8, name="w_planes", align_bytes=64)
         nc.vector.memset(w_planes[:].bitcast(I32), 0)

@@ -26,17 +26,9 @@ BANK_TILES = 2
 BANK_TOKENS = BANK_TILES * P
 ROUND_BANKS = ROUND_TILES // BANK_TILES
 POOLED_AHEAD = 2
-LAST_TILE_GROUPS = 4
 WARM_MATMULS = 4
 
 FLOPS = 2 * TOKENS * A * D + 2 * TOKENS * (PASSES * D) * N_OUT
-
-
-def copy_product(nc, turn, out, in_):
-    if turn % 4 == 3 or turn == TILES + 1:
-        nc.vector.tensor_copy(out=out, in_=in_)
-    else:
-        nc.scalar.copy(out=out, in_=in_)
 
 
 def tile_abstraction_pb_kernel(tc, data, pooled, W_abs, W_merge_words, W_merge_scales, out):
@@ -124,82 +116,102 @@ def tile_abstraction_pb_kernel(tc, data, pooled, W_abs, W_merge_words, W_merge_s
 
         pooled_t = {0: transpose_pooled(0), 1: transpose_pooled(1)}
         data_words = {0: sort_words(0)}
-        x_mx = {}
+        grouped, x_words, x_planes = {}, {}, {}
+
+        def open_round(r):
+            grouped_r = work.tile([P, PASSES, ROUND_TOKENS, PACK], BF16, name="grouped_r", align_bytes=64)
+            words_r = work.tile([P, PASSES, ROUND_TOKENS], U32, name="words_r", align_bytes=64)
+            planes_r = work.tile([P, PASSES, ROUND_TOKENS], U8, name="planes_r", align_bytes=64)
+            grouped[r], x_words[r], x_planes[r] = grouped_r, words_r, planes_r
+
+        def abstract_bank(r, b):
+            tokens = slice(b * BANK_TOKENS, (b + 1) * BANK_TOKENS)
+            abs_t_ps = psum_abs.tile([P, PACK, BANK_TOKENS], BF16, name="abs_t_ps")
+            for t in range(PACK):
+                nc.tensor.matmul(
+                    out=abs_t_ps[:, t, :],
+                    lhsT=w_abs_by_t[:, t, :],
+                    rhs=pooled_t[r][:, tokens],
+                    start=True,
+                    stop=True,
+                )
+            nc.scalar.copy(out=grouped[r][:, 1, tokens, :], in_=abs_t_ps[:].rearrange("p t m -> p m t"))
+
+        def data_bank(r, b):
+            tokens = slice(b * BANK_TOKENS, (b + 1) * BANK_TOKENS)
+            data_t_ps = psum_data.tile([P, BANK_TILES, 2, P], F32, name="data_t_ps")
+            for j in range(BANK_TILES):
+                for u in range(2):
+                    nc.tensor.transpose(
+                        out=data_t_ps[:, j, u, :], in_=data_words[r][b][:, j, u, :], identity=ident_f32[:]
+                    )
+            nc.vector.tensor_copy(
+                out=grouped[r][:, 0, tokens, :].bitcast(F32).rearrange("p (j m) u -> p j m u", j=BANK_TILES),
+                in_=data_t_ps[:].rearrange("p j u m -> p j m u"),
+            )
+
+        def quantise(r, g, first_bank=0, banks=ROUND_BANKS):
+            tokens = slice(first_bank * BANK_TOKENS, (first_bank + banks) * BANK_TOKENS)
+            nc.vector.quantize_mx(
+                out=x_words[r][:, g, tokens].bitcast(FP8X4),
+                scales=x_planes[r][:, g, tokens],
+                in_=grouped[r][:, g, tokens, :].rearrange("p m t -> p (m t)"),
+            )
+
+        def product(token_tile, copy):
+            r, j = divmod(token_tile, ROUND_TILES)
+            tokens = slice(j * P, (j + 1) * P)
+            out_sb = keep.tile([P, N_OUT], F32, name="out%d" % token_tile)
+            out_ps = psum_out.tile([P, N_OUT], F32, name="out_ps", tag="bank")
+            for g in range(PASSES):
+                nc.tensor.matmul_mx(
+                    out=out_ps[:],
+                    lhsT=x_words[r][:, g, tokens].bitcast(FP8X4),
+                    lhsT_scale=x_planes[r][:, g, tokens],
+                    rhs=w_words[:, g, :].bitcast(FP4X4),
+                    rhs_scale=w_planes[:, g, :],
+                    start=(g == 0),
+                    stop=(g == PASSES - 1),
+                )
+            copy(out=out_sb[:], in_=out_ps[:])
+            nc.sync.dma_start(out=out_rows[:, token_tile, :], in_=out_sb[:])
 
         def prepare(r):
-            grouped = work.tile([P, PASSES, ROUND_TOKENS, PACK], BF16, name="grouped", align_bytes=64)
-            x_words = work.tile([P, PASSES, ROUND_TOKENS], U32, name="x_words", align_bytes=64)
-            x_planes = work.tile([P, PASSES, ROUND_TOKENS], U8, name="x_planes", align_bytes=64)
-
-            def abstract_bank(b):
-                tokens = slice(b * BANK_TOKENS, (b + 1) * BANK_TOKENS)
-                abs_t_ps = psum_abs.tile([P, PACK, BANK_TOKENS], BF16, name="abs_t_ps")
-                for t in range(PACK):
-                    nc.tensor.matmul(
-                        out=abs_t_ps[:, t, :],
-                        lhsT=w_abs_by_t[:, t, :],
-                        rhs=pooled_t[r][:, tokens],
-                        start=True,
-                        stop=True,
-                    )
-                nc.scalar.copy(out=grouped[:, 1, tokens, :], in_=abs_t_ps[:].rearrange("p t m -> p m t"))
-
-            def data_bank(b):
-                tokens = slice(b * BANK_TOKENS, (b + 1) * BANK_TOKENS)
-                data_t_ps = psum_data.tile([P, BANK_TILES, 2, P], F32, name="data_t_ps")
-                for j in range(BANK_TILES):
-                    for u in range(2):
-                        nc.tensor.transpose(
-                            out=data_t_ps[:, j, u, :], in_=data_words[r][b][:, j, u, :], identity=ident_f32[:]
-                        )
-                nc.vector.tensor_copy(
-                    out=grouped[:, 0, tokens, :].bitcast(F32).rearrange("p (j m) u -> p j m u", j=BANK_TILES),
-                    in_=data_t_ps[:].rearrange("p j u m -> p j m u"),
-                )
-
-            abstract_bank(0)
+            open_round(r)
+            abstract_bank(r, 0)
             for b in range(ROUND_BANKS):
-                data_bank(b)
+                data_bank(r, b)
             if r + POOLED_AHEAD < ROUNDS:
                 pooled_t[r + POOLED_AHEAD] = transpose_pooled(r + POOLED_AHEAD)
-            abstract_bank(1)
-
-            if r + 1 < ROUNDS:
-                data_words[r + 1] = sort_words(r + 1)
+            abstract_bank(r, 1)
+            data_words[r + 1] = sort_words(r + 1)
             for g in range(PASSES):
-                nc.vector.quantize_mx(
-                    out=x_words[:, g, :].bitcast(FP8X4),
-                    scales=x_planes[:, g, :],
-                    in_=grouped[:, g, :, :].rearrange("p m t -> p (m t)"),
-                )
-            x_mx[r] = (x_words, x_planes)
+                quantise(r, g)
 
         def merge(r):
-            x_words, x_planes = x_mx[r]
             for j in range(ROUND_TILES):
-                token_tile = r * ROUND_TILES + j
-                tokens = slice(j * P, (j + 1) * P)
-                out_sb = keep.tile([P, N_OUT], F32, name="out%d" % token_tile)
-                groups = LAST_TILE_GROUPS if token_tile == TILES - 1 else 1
-                width = N_OUT // groups
-                for c in range(groups):
-                    cols = slice(c * width, (c + 1) * width)
-                    out_ps = psum_out.tile([P, width], F32, name="out_ps", tag="bank")
-                    for g in range(PASSES):
-                        nc.tensor.matmul_mx(
-                            out=out_ps[:],
-                            lhsT=x_words[:, g, tokens].bitcast(FP8X4),
-                            lhsT_scale=x_planes[:, g, tokens],
-                            rhs=w_words[:, g, 2 * c * width : 2 * (c + 1) * width].bitcast(FP4X4),
-                            rhs_scale=w_planes[:, g, cols],
-                            start=(g == 0),
-                            stop=(g == PASSES - 1),
-                        )
-                    copy_product(nc, token_tile + c, out=out_sb[:, cols], in_=out_ps[:])
-                    nc.sync.dma_start(out=out_rows[:, token_tile, cols], in_=out_sb[:, cols])
+                product(r * ROUND_TILES + j, nc.vector.tensor_copy if j == ROUND_TILES - 1 else nc.scalar.copy)
 
         prepare(0)
-        for r in range(ROUNDS):
-            if r + 1 < ROUNDS:
-                prepare(r + 1)
+        for r in range(ROUNDS - 2):
+            prepare(r + 1)
             merge(r)
+
+        last = ROUNDS - 1
+        before = (last - 1) * ROUND_TILES
+        scalar, vector = nc.scalar.copy, nc.vector.tensor_copy
+        open_round(last)
+        data_bank(last, 0)
+        abstract_bank(last, 0)
+        product(before, scalar)
+        quantise(last, 0, first_bank=0, banks=1)
+        data_bank(last, 1)
+        abstract_bank(last, 1)
+        product(before + 1, vector)
+        quantise(last, 1, first_bank=0, banks=1)
+        product(before + 2, scalar)
+        quantise(last, 0, first_bank=1, banks=1)
+        product(before + 3, vector)
+        quantise(last, 1, first_bank=1, banks=1)
+        for j in range(ROUND_TILES):
+            product(last * ROUND_TILES + j, scalar if j % 2 == 0 else vector)

from contextlib import ExitStack

import concourse.mybir as mybir
from concourse.masks import make_identity

BF16 = mybir.dt.bfloat16
F32 = mybir.dt.float32
I32 = mybir.dt.int32
U32 = mybir.dt.uint32
U8 = mybir.dt.uint8
FP8X4 = mybir.dt.float8_e4m3fn_x4
FP4X4 = mybir.dt.float4_e2m1fn_x4

P = 128
PACK = 4
TOKENS = 4 * 1024
D = 512
A = 128
N_OUT = 512
PASSES = 2
TILES = TOKENS // P
ROUND_TILES = 4
ROUNDS = TILES // ROUND_TILES
ROUND_TOKENS = ROUND_TILES * P
BANK_TILES = 2
BANK_TOKENS = BANK_TILES * P
ROUND_BANKS = ROUND_TILES // BANK_TILES
POOLED_AHEAD = 2
WARM_MATMULS = 4

FLOPS = 2 * TOKENS * A * D + 2 * TOKENS * (PASSES * D) * N_OUT


def tile_abstraction_pb_kernel(tc, data, pooled, W_abs, W_merge_words, W_merge_scales, out):
    nc = tc.nc
    data_rows = data.flatten_outer_dims().rearrange("(p i) k -> p i k", i=TILES)
    pooled_rows = pooled.flatten_outer_dims().rearrange("(p i) a -> p i a", i=TILES)
    out_rows = out.flatten_outer_dims().rearrange("(p i) n -> p i n", i=TILES)

    with ExitStack() as ctx:
        ctx.enter_context(tc.manual_schedule())
        keep = ctx.enter_context(tc.tile_pool(name="keep", bufs=1))
        work = ctx.enter_context(tc.tile_pool(name="work", bufs=3))
        sorted_pool = ctx.enter_context(tc.tile_pool(name="sorted_pool", bufs=2 * ROUND_BANKS))
        psum_data = ctx.enter_context(tc.psum_pool(name="psum_data", bufs=2))
        psum_abs = ctx.enter_context(tc.psum_pool(name="psum_abs", bufs=2))
        psum_out = ctx.enter_context(tc.psum_pool(name="psum_out", bufs=4))

        zeros = keep.tile([P, N_OUT], BF16, name="zeros")
        nc.vector.memset(zeros[:], 0.0)
        warm_ps = psum_out.tile([P, N_OUT], F32, name="warm_ps", tag="bank")
        for i in range(WARM_MATMULS):
            nc.tensor.matmul(out=warm_ps[:], lhsT=zeros[:, 0:P], rhs=zeros[:], start=True, stop=True)

        w_planes = keep.tile([P, PASSES, N_OUT], U8, name="w_planes", align_bytes=64)
        nc.vector.memset(w_planes[:].bitcast(I32), 0)
        ident_bf16 = keep.tile([P, P], BF16, name="ident_bf16")
        make_identity(nc, ident_bf16[:])
        ident_f32 = keep.tile([P, P], F32, name="ident_f32")
        make_identity(nc, ident_f32[:])

        pooled_sb = [keep.tile([P, ROUND_TILES, A], BF16, name="pooled%d" % r) for r in range(ROUNDS)]
        data_sb = [
            [keep.tile([P, BANK_TILES, D], BF16, name="data%d_%d" % (r, b)) for b in range(ROUND_BANKS)]
            for r in range(ROUNDS)
        ]
        w_abs_sb = keep.tile([A, D], BF16, name="w_abs_sb")
        w_words = keep.tile([P, PASSES, 2 * N_OUT], U8, name="w_words", align_bytes=64)

        def load_pooled(r):
            tiles = slice(r * ROUND_TILES, (r + 1) * ROUND_TILES)
            nc.sync.dma_start(out=pooled_sb[r][:], in_=pooled_rows[:, tiles, :])

        def load_round(r):
            for b in range(ROUND_BANKS):
                first_tile = r * ROUND_TILES + b * BANK_TILES
                nc.sync.dma_start(out=data_sb[r][b][:], in_=data_rows[:, first_tile : first_tile + BANK_TILES, :])
            if r + POOLED_AHEAD < ROUNDS:
                load_pooled(r + POOLED_AHEAD)

        load_pooled(0)
        nc.sync.dma_start(out=w_abs_sb[:], in_=W_abs)
        load_pooled(1)
        load_round(0)
        load_round(1)
        nc.sync.dma_start(
            out=w_words[:].bitcast(I32),
            in_=W_merge_words.bitcast(I32).rearrange("g p w -> p g w"),
        )
        scale_rows = W_merge_scales.bitcast(I32).rearrange("g (q s) w -> s q g w", s=4)
        for s in range(4):
            nc.sync.dma_start(out=w_planes[:].bitcast(I32)[s:P:32, :, :], in_=scale_rows[s])
        for r in range(2, ROUNDS):
            load_round(r)

        w_abs_by_t = keep.tile([A, PACK, P], BF16, name="w_abs_by_t")
        nc.vector.tensor_copy(out=w_abs_by_t[:], in_=w_abs_sb[:].rearrange("a (p t) -> a t p", t=PACK))

        def transpose_pooled(r):
            pooled_t_ps = psum_out.tile([A, ROUND_TILES, P], BF16, name="pooled_t_ps", tag="bank")
            for j in range(ROUND_TILES):
                nc.tensor.transpose(out=pooled_t_ps[:, j, :], in_=pooled_sb[r][:, j, :], identity=ident_bf16[:])
            transposed = work.tile([A, ROUND_TOKENS], BF16, name="transposed")
            nc.scalar.copy(out=transposed[:], in_=pooled_t_ps[:].rearrange("a j m -> a (j m)"))
            return transposed

        def sort_words(r):
            banks = []
            for b in range(ROUND_BANKS):
                by_half = sorted_pool.tile([P, BANK_TILES, 2, P], F32, name="by_half")
                nc.vector.tensor_copy(
                    out=by_half[:], in_=data_sb[r][b][:].bitcast(F32).rearrange("m j (p u) -> m j u p", u=2)
                )
                banks.append(by_half)
            return banks

        pooled_t = {0: transpose_pooled(0), 1: transpose_pooled(1)}
        data_words = {0: sort_words(0)}
        grouped, x_words, x_planes = {}, {}, {}

        def open_round(r):
            grouped_r = work.tile([P, PASSES, ROUND_TOKENS, PACK], BF16, name="grouped_r", align_bytes=64)
            words_r = work.tile([P, PASSES, ROUND_TOKENS], U32, name="words_r", align_bytes=64)
            planes_r = work.tile([P, PASSES, ROUND_TOKENS], U8, name="planes_r", align_bytes=64)
            grouped[r], x_words[r], x_planes[r] = grouped_r, words_r, planes_r

        def abstract_bank(r, b):
            tokens = slice(b * BANK_TOKENS, (b + 1) * BANK_TOKENS)
            abs_t_ps = psum_abs.tile([P, PACK, BANK_TOKENS], BF16, name="abs_t_ps")
            for t in range(PACK):
                nc.tensor.matmul(
                    out=abs_t_ps[:, t, :],
                    lhsT=w_abs_by_t[:, t, :],
                    rhs=pooled_t[r][:, tokens],
                    start=True,
                    stop=True,
                )
            nc.scalar.copy(out=grouped[r][:, 1, tokens, :], in_=abs_t_ps[:].rearrange("p t m -> p m t"))

        def data_bank(r, b):
            tokens = slice(b * BANK_TOKENS, (b + 1) * BANK_TOKENS)
            data_t_ps = psum_data.tile([P, BANK_TILES, 2, P], F32, name="data_t_ps")
            for j in range(BANK_TILES):
                for u in range(2):
                    nc.tensor.transpose(
                        out=data_t_ps[:, j, u, :], in_=data_words[r][b][:, j, u, :], identity=ident_f32[:]
                    )
            nc.vector.tensor_copy(
                out=grouped[r][:, 0, tokens, :].bitcast(F32).rearrange("p (j m) u -> p j m u", j=BANK_TILES),
                in_=data_t_ps[:].rearrange("p j u m -> p j m u"),
            )

        def quantise(r, g, first_bank=0, banks=ROUND_BANKS):
            tokens = slice(first_bank * BANK_TOKENS, (first_bank + banks) * BANK_TOKENS)
            nc.vector.quantize_mx(
                out=x_words[r][:, g, tokens].bitcast(FP8X4),
                scales=x_planes[r][:, g, tokens],
                in_=grouped[r][:, g, tokens, :].rearrange("p m t -> p (m t)"),
            )

        def product(token_tile, copy):
            r, j = divmod(token_tile, ROUND_TILES)
            tokens = slice(j * P, (j + 1) * P)
            out_sb = keep.tile([P, N_OUT], F32, name="out%d" % token_tile)
            out_ps = psum_out.tile([P, N_OUT], F32, name="out_ps", tag="bank")
            for g in range(PASSES):
                nc.tensor.matmul_mx(
                    out=out_ps[:],
                    lhsT=x_words[r][:, g, tokens].bitcast(FP8X4),
                    lhsT_scale=x_planes[r][:, g, tokens],
                    rhs=w_words[:, g, :].bitcast(FP4X4),
                    rhs_scale=w_planes[:, g, :],
                    start=(g == 0),
                    stop=(g == PASSES - 1),
                )
            copy(out=out_sb[:], in_=out_ps[:])
            nc.sync.dma_start(out=out_rows[:, token_tile, :], in_=out_sb[:])

        def prepare(r):
            open_round(r)
            abstract_bank(r, 0)
            for b in range(ROUND_BANKS):
                data_bank(r, b)
            if r + POOLED_AHEAD < ROUNDS:
                pooled_t[r + POOLED_AHEAD] = transpose_pooled(r + POOLED_AHEAD)
            abstract_bank(r, 1)
            data_words[r + 1] = sort_words(r + 1)
            for g in range(PASSES):
                quantise(r, g)

        def merge(r):
            for j in range(ROUND_TILES):
                product(r * ROUND_TILES + j, nc.vector.tensor_copy if j == ROUND_TILES - 1 else nc.scalar.copy)

        prepare(0)
        for r in range(ROUNDS - 2):
            prepare(r + 1)
            merge(r)

        last = ROUNDS - 1
        before = (last - 1) * ROUND_TILES
        scalar, vector = nc.scalar.copy, nc.vector.tensor_copy
        open_round(last)
        data_bank(last, 0)
        abstract_bank(last, 0)
        product(before, scalar)
        quantise(last, 0, first_bank=0, banks=1)
        data_bank(last, 1)
        abstract_bank(last, 1)
        product(before + 1, vector)
        quantise(last, 1, first_bank=0, banks=1)
        product(before + 2, scalar)
        quantise(last, 0, first_bank=1, banks=1)
        product(before + 3, vector)
        quantise(last, 1, first_bank=1, banks=1)
        for j in range(ROUND_TILES):
            product(last * ROUND_TILES + j, scalar if j % 2 == 0 else vector)
